import numpy as np
import ml_dtypes


def mxq(x, axis, fmt="e4m3"):
    dtype, down = {"e4m3": (ml_dtypes.float8_e4m3fn, 7), "e5m2": (ml_dtypes.float8_e5m2, 14)}[fmt]
    v = np.moveaxis(np.asarray(x, np.float32).astype(ml_dtypes.bfloat16).astype(np.float64), axis, -1)
    blocks = v.reshape(v.shape[:-1] + (-1, 32))
    amax = np.abs(blocks).max(-1, keepdims=True)
    byte = np.maximum(np.where(amax > 0, np.frexp(amax)[1] - 1 + 127, 0) - down, 1)
    scale = np.exp2(byte - 127.0)
    codes = (blocks / scale).astype(np.float32).astype(dtype).astype(np.float64)
    return np.moveaxis((codes * scale).reshape(v.shape), -1, axis)


WIDE = False


def mx_kscale(k):
    if not WIDE:
        return np.ones(k)
    levels = np.array([10, -10, 5, -5, 0])
    a = np.random.permutation(np.resize(levels, k // 512 * 4)).reshape(k // 512, 4)
    idx = np.arange(k)
    return np.exp2(a[idx // 512, idx % 128 // 32])


BF16 = ml_dtypes.bfloat16


def bf(x):
    return np.asarray(x, np.float32).astype(BF16)


def f64(x):
    return np.asarray(x).astype(np.float64)


B, CB, CD, H, W = 4, 4, 512, 16, 16
C = CB * CD


def erf(z):
    z = np.clip(z, -6.0, 6.0)
    z2 = 2.0 * z * z
    term = z.copy()
    tot = z.copy()
    for n in range(1, 101):
        term *= z2
        term /= 2 * n + 1
        tot += term
    return 2.0 / np.sqrt(np.pi) * np.exp(-z * z) * tot


def gelu_erf(v):
    return 0.5 * v * (1.0 + erf(v / np.sqrt(2.0)))


def setup_inputs():
    s = mx_kscale(CD)
    s = s / s.max()
    sc = np.tile(s, CB)
    return {"x": bf(np.random.standard_normal((B, C, H, W)) * sc[None, :, None, None]),
            "wc": bf(np.random.standard_normal((CB, CD, CD)) / np.sqrt(CD) / s[None, :, None])}


def reference(x, wc):
    x = f64(x)
    xr = np.transpose(x, (0, 2, 3, 1)).reshape(B, H, W, CB, CD)
    xb = xr.transpose(3, 0, 1, 2, 4).reshape(CB, B * H * W, CD)
    out = mxq(xb, 2, "e4m3") @ mxq(f64(wc), 1, "e4m3")
    out = out.reshape(CB, B, H, W, CD).transpose(1, 2, 3, 0, 4)
    out = out.reshape(B, H, W, C).transpose(0, 3, 1, 2)
    return gelu_erf(x + out)

@@ -1,0 +1,179 @@
+from contextlib import ExitStack
+
+import concourse.mybir as mybir
+
+BF16 = mybir.dt.bfloat16
+F32 = mybir.dt.float32
+U32 = mybir.dt.uint32
+U8 = mybir.dt.uint8
+FP8X4 = mybir.dt.float8_e4m3fn_x4
+GELU = mybir.ActivationFunctionType.Gelu
+ADD = mybir.AluOpType.add
+
+P = 128
+B = 4
+CB = 4
+CD = 512
+HW = 256
+PACK = 4
+NV = B * CB
+SLAB = PACK * HW
+
+FLOPS = 2 * CB * B * HW * CD * CD
+
+X_LEAD = 4
+W_LEAD = 7
+W0_VECTOR_M = 84
+FINE_TAIL = 2
+
+
+def scalar_groups(v):
+    return 16 if v < 12 else 32
+
+
+def tile_spectralchannelmixing_kernel(tc, x, wc, out):
+    nc = tc.nc
+    with ExitStack() as ctx:
+        keep = ctx.enter_context(tc.tile_pool(name="keep", bufs=1))
+        banks = ctx.enter_context(tc.psum_pool(name="banks", bufs=8))
+        ctx.enter_context(tc.manual_schedule())
+
+        w_raw = [keep.tile([P, PACK * CD], BF16, name="w_raw%d" % i) for i in range(CB)]
+        w_grp = [keep.tile([P, PACK * CD], BF16, name="w_grp%d" % i, align_bytes=64) for i in range(CB)]
+        w_code = [keep.tile([P, CD], U32, name="w_code%d" % i, align_bytes=64) for i in range(CB)]
+        w_scale = [keep.tile([P, CD], U8, name="w_scale%d" % i, align_bytes=64) for i in range(CB)]
+        x_grp = [keep.tile([P, SLAB], BF16, name="x_grp%d" % v, align_bytes=64) for v in range(NV)]
+        x_code = [keep.tile([P, HW], U32, name="x_code%d" % v, align_bytes=64) for v in range(NV)]
+        x_scale = [keep.tile([P, HW], U8, name="x_scale%d" % v, align_bytes=64) for v in range(NV)]
+        res = [keep.tile([P, SLAB], F32, name="res%d" % v) for v in range(NV)]
+        x_raw = []
+        acc = {}
+
+        def channels(i):
+            return slice(i * CD, (i + 1) * CD)
+
+        def load_w(i):
+            nc.sync.dma_start(out=w_raw[i][:], in_=wc[i].rearrange("(p j) o -> p (j o)", j=PACK))
+
+        def load_x_one(v):
+            one = keep.tile([P, SLAB], BF16, name="x_raw%d" % v)
+            nc.sync.dma_start(
+                out=one[:],
+                in_=x[v % B, channels(v // B)].rearrange("(p j) h w -> p (j h w)", j=PACK),
+            )
+            x_raw.append(one[:])
+
+        def load_x_pair(v):
+            pair = keep.tile([P, 2, SLAB], BF16, name="x_raw%d" % v)
+            b = v % B
+            nc.sync.dma_start(
+                out=pair[:],
+                in_=x[b : b + 2, channels(v // B)].rearrange("b (p j) h w -> p b (j h w)", j=PACK),
+            )
+            x_raw.append(pair[:, 0, :])
+            x_raw.append(pair[:, 1, :])
+
+        def regroup_x(copy, v, c0, c1):
+            copy(
+                out=x_grp[v][:].rearrange("p (c i t) -> p c t i", i=4, t=PACK)[:, c0:c1],
+                in_=x_raw[v].rearrange("p (t c i) -> p c t i", t=PACK, i=4)[:, c0:c1],
+            )
+
+        def regroup_x_scalar(v):
+            if v < NV:
+                regroup_x(nc.scalar.copy, v, HW // 4 - scalar_groups(v), HW // 4)
+
+        def regroup_x_vector(v):
+            if v < NV:
+                regroup_x(nc.vector.tensor_copy, v, 0, HW // 4 - scalar_groups(v))
+
+        def regroup_w(copy, i, m0, m1):
+            copy(
+                out=w_grp[i][:].rearrange("p (t m j) -> p m j t", t=4, j=PACK)[:, m0:m1],
+                in_=w_raw[i][:].rearrange("p (j m t) -> p m j t", j=PACK, t=4)[:, m0:m1],
+            )
+
+        def regroup_w_quarter(n):
+            if n < 4 * CB:
+                regroup_w(nc.scalar.copy, n // 4, 32 * (n % 4), 32 * (n % 4) + 32)
+
+        def quantise_w(i):
+            nc.vector.quantize_mx(out=w_code[i][:].bitcast(FP8X4), scales=w_scale[i][:], in_=w_grp[i][:])
+
+        def quantise_x(v):
+            nc.vector.quantize_mx(out=x_code[v][:].bitcast(FP8X4), scales=x_scale[v][:], in_=x_grp[v][:])
+
+        def multiply(v):
+            i = v // B
+            for h in range(2):
+                bank = banks.tile([P, 2, HW], F32, name="acc", tag="acc")
+                acc[(v, h)] = bank
+                for e in range(2):
+                    cols = slice((2 * h + e) * P, (2 * h + e + 1) * P)
+                    nc.tensor.matmul_mx(
+                        out=bank[:, e, :],
+                        lhsT=w_code[i][:, cols].bitcast(FP8X4),
+                        lhsT_scale=w_scale[i][:, cols],
+                        rhs=x_code[v][:].bitcast(FP8X4),
+                        rhs_scale=x_scale[v][:],
+                        start=True,
+                        stop=True,
+                    )
+
+        def finish(v):
+            dst = out[v % B, channels(v // B)].rearrange("(p t) h w -> p (t h w)", t=4)
+            half = SLAB // 2
+            for h in range(2):
+                part = slice(h * half, (h + 1) * half)
+                nc.vector.tensor_tensor(
+                    out=res[v][:, part],
+                    in0=acc[(v, h)][:].rearrange("p e q -> p (e q)"),
+                    in1=x_raw[v][:, part],
+                    op=ADD,
+                )
+            if v >= NV - FINE_TAIL:
+                for h in range(2):
+                    part = slice(h * half, (h + 1) * half)
+                    nc.scalar.activation(out=res[v][:, part], in_=res[v][:, part], func=GELU)
+                    nc.sync.dma_start(out=dst[:, part], in_=res[v][:, part])
+            else:
+                nc.scalar.activation(out=res[v][:], in_=res[v][:], func=GELU)
+                nc.sync.dma_start(out=dst, in_=res[v][:])
+
+        warm = keep.tile([P, 1], F32, name="warm")
+        nc.vector.memset(warm[:], 0.0)
+        nc.scalar.activation(out=warm[:], in_=warm[:], func=GELU)
+
+        load_x_one(0)
+        load_w(0)
+        load_x_one(1)
+        load_x_pair(2)
+        for i in range(1, CB):
+            load_w(i)
+            load_x_pair(B * i)
+            load_x_pair(B * i + 2)
+
+        regroup_x_scalar(0)
+        regroup_x_vector(0)
+        regroup_w(nc.vector.tensor_copy, 0, 0, W0_VECTOR_M)
+        regroup_w(nc.scalar.copy, 0, W0_VECTOR_M, P)
+        regroup_x_scalar(1)
+        regroup_x_vector(1)
+        quantise_x(0)
+        quantise_w(0)
+        multiply(0)
+        for v in range(2, X_LEAD):
+            regroup_x_scalar(v)
+        for n in range(4, W_LEAD):
+            regroup_w_quarter(n)
+
+        for v in range(NV):
+            regroup_x_scalar(v + X_LEAD)
+            regroup_w_quarter(v + W_LEAD)
+            if v + 1 < NV:
+                if (v + 1) % B == 0:
+                    quantise_w((v + 1) // B)
+                quantise_x(v + 1)
+                multiply(v + 1)
+            regroup_x_vector(v + 2)
+            finish(v)

@@ -9,6 +9,7 @@ U8 = mybir.dt.uint8
 FP8X4 = mybir.dt.float8_e4m3fn_x4
 GELU = mybir.ActivationFunctionType.Gelu
 ADD = mybir.AluOpType.add
+MULT = mybir.AluOpType.mult
 
 P = 128
 B = 4
@@ -21,20 +22,25 @@ SLAB = PACK * HW
 
 FLOPS = 2 * CB * B * HW * CD * CD
 
-X_LEAD = 4
-W_LEAD = 7
+W_LEAD = 6
 W0_VECTOR_M = 84
 FINE_TAIL = 2
+FIRST_POOL_SLAB = 3
+
+
+def on_pool(v):
+    return v % 2 == 1 and v >= FIRST_POOL_SLAB
 
 
 def scalar_groups(v):
-    return 16 if v < 12 else 32
+    return 16 if v == 1 else 24
 
 
 def tile_spectralchannelmixing_kernel(tc, x, wc, out):
     nc = tc.nc
     with ExitStack() as ctx:
         keep = ctx.enter_context(tc.tile_pool(name="keep", bufs=1))
+        stage = ctx.enter_context(tc.tile_pool(name="stage", bufs=1))
         banks = ctx.enter_context(tc.psum_pool(name="banks", bufs=8))
         ctx.enter_context(tc.manual_schedule())
 
@@ -42,11 +48,11 @@ def tile_spectralchannelmixing_kernel(tc, x, wc, out):
         w_grp = [keep.tile([P, PACK * CD], BF16, name="w_grp%d" % i, align_bytes=64) for i in range(CB)]
         w_code = [keep.tile([P, CD], U32, name="w_code%d" % i, align_bytes=64) for i in range(CB)]
         w_scale = [keep.tile([P, CD], U8, name="w_scale%d" % i, align_bytes=64) for i in range(CB)]
-        x_grp = [keep.tile([P, SLAB], BF16, name="x_grp%d" % v, align_bytes=64) for v in range(NV)]
         x_code = [keep.tile([P, HW], U32, name="x_code%d" % v, align_bytes=64) for v in range(NV)]
         x_scale = [keep.tile([P, HW], U8, name="x_scale%d" % v, align_bytes=64) for v in range(NV)]
         res = [keep.tile([P, SLAB], F32, name="res%d" % v) for v in range(NV)]
         x_raw = []
+        x_grp = {}
         acc = {}
 
         def channels(i):
@@ -73,19 +79,38 @@ def tile_spectralchannelmixing_kernel(tc, x, wc, out):
             x_raw.append(pair[:, 0, :])
             x_raw.append(pair[:, 1, :])
 
+        def grouped(v):
+            if v not in x_grp:
+                if v % 2 == 1:
+                    x_grp[v] = stage.tile([P, SLAB], BF16, name="odd_grp", tag="odd_grp", align_bytes=64)
+                else:
+                    x_grp[v] = keep.tile([P, SLAB], BF16, name="x_grp%d" % v, align_bytes=64)
+            return x_grp[v]
+
         def regroup_x(copy, v, c0, c1):
             copy(
-                out=x_grp[v][:].rearrange("p (c i t) -> p c t i", i=4, t=PACK)[:, c0:c1],
+                out=grouped(v)[:].rearrange("p (c i t) -> p c t i", i=4, t=PACK)[:, c0:c1],
                 in_=x_raw[v].rearrange("p (t c i) -> p c t i", t=PACK, i=4)[:, c0:c1],
             )
 
         def regroup_x_scalar(v):
-            if v < NV:
+            if v < NV and not on_pool(v):
                 regroup_x(nc.scalar.copy, v, HW // 4 - scalar_groups(v), HW // 4)
 
         def regroup_x_vector(v):
-            if v < NV:
+            if v < NV and not on_pool(v):
                 regroup_x(nc.vector.tensor_copy, v, 0, HW // 4 - scalar_groups(v))
+
+        def regroup_x_pool(v):
+            if v < NV and on_pool(v):
+                nc.gpsimd.tensor_scalar(
+                    out=grouped(v)[:].rearrange("p (q t) -> p q t", t=PACK),
+                    in0=x_raw[v].rearrange("p (t q) -> p q t", t=PACK),
+                    scalar1=1.0,
+                    scalar2=0.0,
+                    op0=MULT,
+                    op1=ADD,
+                )
 
         def regroup_w(copy, i, m0, m1):
             copy(
@@ -101,7 +126,7 @@ def tile_spectralchannelmixing_kernel(tc, x, wc, out):
             nc.vector.quantize_mx(out=w_code[i][:].bitcast(FP8X4), scales=w_scale[i][:], in_=w_grp[i][:])
 
         def quantise_x(v):
-            nc.vector.quantize_mx(out=x_code[v][:].bitcast(FP8X4), scales=x_scale[v][:], in_=x_grp[v][:])
+            nc.vector.quantize_mx(out=x_code[v][:].bitcast(FP8X4), scales=x_scale[v][:], in_=grouped(v)[:])
 
         def multiply(v):
             i = v // B
@@ -162,18 +187,25 @@ def tile_spectralchannelmixing_kernel(tc, x, wc, out):
         quantise_x(0)
         quantise_w(0)
         multiply(0)
-        for v in range(2, X_LEAD):
-            regroup_x_scalar(v)
+        regroup_x_scalar(2)
+        regroup_x_vector(2)
         for n in range(4, W_LEAD):
             regroup_w_quarter(n)
 
-        for v in range(NV):
-            regroup_x_scalar(v + X_LEAD)
-            regroup_w_quarter(v + W_LEAD)
-            if v + 1 < NV:
-                if (v + 1) % B == 0:
-                    quantise_w((v + 1) // B)
-                quantise_x(v + 1)
-                multiply(v + 1)
-            regroup_x_vector(v + 2)
-            finish(v)
+        for a in range(0, NV, 2):
+            b = a + 1
+            regroup_x_scalar(a + 4)
+            regroup_w_quarter(W_LEAD + a)
+            regroup_w_quarter(W_LEAD + a + 1)
+            regroup_x_vector(a + 4)
+            if a + 2 < NV:
+                if (a + 2) % B == 0:
+                    quantise_w((a + 2) // B)
+                quantise_x(a + 2)
+            quantise_x(b)
+            multiply(b)
+            if a + 2 < NV:
+                multiply(a + 2)
+            regroup_x_pool(b + 2)
+            finish(a)
+            finish(b)

@@ -25,7 +25,7 @@ FLOPS = 2 * CB * B * HW * CD * CD
 W_LEAD = 6
 W0_VECTOR_M = 84
 FINE_TAIL = 2
-FIRST_POOL_SLAB = 3
+FIRST_POOL_SLAB = 5
 
 
 def on_pool(v):
@@ -33,7 +33,7 @@ def on_pool(v):
 
 
 def scalar_groups(v):
-    return 16 if v == 1 else 24
+    return 16 if v in (1, 3) else 24
 
 
 def tile_spectralchannelmixing_kernel(tc, x, wc, out):
@@ -189,6 +189,10 @@ def tile_spectralchannelmixing_kernel(tc, x, wc, out):
         multiply(0)
         regroup_x_scalar(2)
         regroup_x_vector(2)
+        quantise_x(1)
+        multiply(1)
+        regroup_x_scalar(3)
+        regroup_x_vector(3)
         for n in range(4, W_LEAD):
             regroup_w_quarter(n)
 
@@ -202,10 +206,9 @@ def tile_spectralchannelmixing_kernel(tc, x, wc, out):
                 if (a + 2) % B == 0:
                     quantise_w((a + 2) // B)
                 quantise_x(a + 2)
-            quantise_x(b)
-            multiply(b)
-            if a + 2 < NV:
+                quantise_x(b + 2)
                 multiply(a + 2)
-            regroup_x_pool(b + 2)
+                multiply(b + 2)
+            regroup_x_pool(b + 4)
             finish(a)
             finish(b)

@@ -19,13 +19,15 @@ HW = 256
 PACK = 4
 NV = B * CB
 SLAB = PACK * HW
+GROUPS = HW // 4
 
 FLOPS = 2 * CB * B * HW * CD * CD
 
 W_LEAD = 6
-W0_VECTOR_M = 84
-FINE_TAIL = 2
+W0_VECTOR_M = 68
+FINE_GELU = 4
 FIRST_POOL_SLAB = 5
+LAST_CUTS = (0, 512, 768, 1024)
 
 
 def on_pool(v):
@@ -33,7 +35,11 @@ def on_pool(v):
 
 
 def scalar_groups(v):
-    return 16 if v in (1, 3) else 24
+    if v < 2:
+        return 0
+    if v < 4:
+        return 16
+    return 24
 
 
 def tile_spectralchannelmixing_kernel(tc, x, wc, out):
@@ -94,12 +100,12 @@ def tile_spectralchannelmixing_kernel(tc, x, wc, out):
             )
 
         def regroup_x_scalar(v):
-            if v < NV and not on_pool(v):
-                regroup_x(nc.scalar.copy, v, HW // 4 - scalar_groups(v), HW // 4)
+            if v < NV and not on_pool(v) and scalar_groups(v) > 0:
+                regroup_x(nc.scalar.copy, v, GROUPS - scalar_groups(v), GROUPS)
 
         def regroup_x_vector(v):
             if v < NV and not on_pool(v):
-                regroup_x(nc.vector.tensor_copy, v, 0, HW // 4 - scalar_groups(v))
+                regroup_x(nc.vector.tensor_copy, v, 0, GROUPS - scalar_groups(v))
 
         def regroup_x_pool(v):
             if v < NV and on_pool(v):
@@ -131,12 +137,12 @@ def tile_spectralchannelmixing_kernel(tc, x, wc, out):
         def multiply(v):
             i = v // B
             for h in range(2):
-                bank = banks.tile([P, 2, HW], F32, name="acc", tag="acc")
+                bank = banks.tile([P, 2 * HW], F32, name="acc", tag="acc")
                 acc[(v, h)] = bank
                 for e in range(2):
                     cols = slice((2 * h + e) * P, (2 * h + e + 1) * P)
                     nc.tensor.matmul_mx(
-                        out=bank[:, e, :],
+                        out=bank[:, e * HW : (e + 1) * HW],
                         lhsT=w_code[i][:, cols].bitcast(FP8X4),
                         lhsT_scale=w_scale[i][:, cols],
                         rhs=x_code[v][:].bitcast(FP8X4),
@@ -148,21 +154,25 @@ def tile_spectralchannelmixing_kernel(tc, x, wc, out):
         def finish(v):
             dst = out[v % B, channels(v // B)].rearrange("(p t) h w -> p (t h w)", t=4)
             half = SLAB // 2
-            for h in range(2):
-                part = slice(h * half, (h + 1) * half)
+            if v == NV - 1:
+                cuts = LAST_CUTS
+            elif v >= NV - FINE_GELU:
+                cuts = (0, half, SLAB)
+            else:
+                cuts = (0, SLAB)
+            add_cuts = sorted(set(cuts + (half,)))
+            for lo, hi in zip(add_cuts[:-1], add_cuts[1:]):
                 nc.vector.tensor_tensor(
-                    out=res[v][:, part],
-                    in0=acc[(v, h)][:].rearrange("p e q -> p (e q)"),
-                    in1=x_raw[v][:, part],
+                    out=res[v][:, lo:hi],
+                    in0=acc[(v, lo // half)][:, lo % half : lo % half + hi - lo],
+                    in1=x_raw[v][:, lo:hi],
                     op=ADD,
                 )
-            if v >= NV - FINE_TAIL:
-                for h in range(2):
-                    part = slice(h * half, (h + 1) * half)
-                    nc.scalar.activation(out=res[v][:, part], in_=res[v][:, part], func=GELU)
-                    nc.sync.dma_start(out=dst[:, part], in_=res[v][:, part])
-            else:
-                nc.scalar.activation(out=res[v][:], in_=res[v][:], func=GELU)
+            for lo, hi in zip(cuts[:-1], cuts[1:]):
+                nc.scalar.activation(out=res[v][:, lo:hi], in_=res[v][:, lo:hi], func=GELU)
+                if v == NV - 1:
+                    nc.sync.dma_start(out=dst[:, lo:hi], in_=res[v][:, lo:hi])
+            if v < NV - 1:
                 nc.sync.dma_start(out=dst, in_=res[v][:])
 
         warm = keep.tile([P, 1], F32, name="warm")
@@ -170,8 +180,8 @@ def tile_spectralchannelmixing_kernel(tc, x, wc, out):
         nc.scalar.activation(out=warm[:], in_=warm[:], func=GELU)
 
         load_x_one(0)
-        load_w(0)
         load_x_one(1)
+        load_w(0)
         load_x_pair(2)
         for i in range(1, CB):
             load_w(i)
@@ -180,16 +190,16 @@ def tile_spectralchannelmixing_kernel(tc, x, wc, out):
 
         regroup_x_scalar(0)
         regroup_x_vector(0)
-        regroup_w(nc.vector.tensor_copy, 0, 0, W0_VECTOR_M)
-        regroup_w(nc.scalar.copy, 0, W0_VECTOR_M, P)
         regroup_x_scalar(1)
         regroup_x_vector(1)
         quantise_x(0)
-        quantise_w(0)
-        multiply(0)
+        quantise_x(1)
+        regroup_w(nc.vector.tensor_copy, 0, 0, W0_VECTOR_M)
+        regroup_w(nc.scalar.copy, 0, W0_VECTOR_M, P)
         regroup_x_scalar(2)
         regroup_x_vector(2)
-        quantise_x(1)
+        quantise_w(0)
+        multiply(0)
         multiply(1)
         regroup_x_scalar(3)
         regroup_x_vector(3)
@@ -201,7 +211,10 @@ def tile_spectralchannelmixing_kernel(tc, x, wc, out):
             regroup_x_scalar(a + 4)
             regroup_w_quarter(W_LEAD + a)
             regroup_w_quarter(W_LEAD + a + 1)
-            regroup_x_vector(a + 4)
+            if a == 2:
+                regroup_x_vector(4)
+            if a >= 2:
+                regroup_x_vector(a + 4)
             if a + 2 < NV:
                 if (a + 2) % B == 0:
                     quantise_w((a + 2) // B)

@@ -24,9 +24,9 @@ GROUPS = HW // 4
 FLOPS = 2 * CB * B * HW * CD * CD
 
 W_LEAD = 6
-W0_VECTOR_M = 68
 FINE_GELU = 4
 FIRST_POOL_SLAB = 5
+FIRST_SHARED_SLAB = 6
 LAST_CUTS = (0, 512, 768, 1024)
 
 
@@ -34,10 +34,16 @@ def on_pool(v):
     return v % 2 == 1 and v >= FIRST_POOL_SLAB
 
 
+def pool_groups(v):
+    if v % 2 == 0 and v >= FIRST_SHARED_SLAB:
+        return 24
+    return 0
+
+
 def scalar_groups(v):
     if v < 2:
-        return 0
-    if v < 4:
+        return 20
+    if pool_groups(v) > 0:
         return 16
     return 24
 
@@ -105,13 +111,15 @@ def tile_spectralchannelmixing_kernel(tc, x, wc, out):
 
         def regroup_x_vector(v):
             if v < NV and not on_pool(v):
-                regroup_x(nc.vector.tensor_copy, v, 0, GROUPS - scalar_groups(v))
+                regroup_x(nc.vector.tensor_copy, v, 0, GROUPS - scalar_groups(v) - pool_groups(v))
 
         def regroup_x_pool(v):
-            if v < NV and on_pool(v):
+            if v < NV and (on_pool(v) or pool_groups(v) > 0):
+                q1 = HW if on_pool(v) else 4 * (GROUPS - scalar_groups(v))
+                q0 = 0 if on_pool(v) else q1 - 4 * pool_groups(v)
                 nc.gpsimd.tensor_scalar(
-                    out=grouped(v)[:].rearrange("p (q t) -> p q t", t=PACK),
-                    in0=x_raw[v].rearrange("p (t q) -> p q t", t=PACK),
+                    out=grouped(v)[:].rearrange("p (q t) -> p q t", t=PACK)[:, q0:q1],
+                    in0=x_raw[v].rearrange("p (t q) -> p q t", t=PACK)[:, q0:q1],
                     scalar1=1.0,
                     scalar2=0.0,
                     op0=MULT,
@@ -127,6 +135,19 @@ def tile_spectralchannelmixing_kernel(tc, x, wc, out):
         def regroup_w_quarter(n):
             if n < 4 * CB:
                 regroup_w(nc.scalar.copy, n // 4, 32 * (n % 4), 32 * (n % 4) + 32)
+
+        def regroup_w_tiles(copy, i, t0, t1):
+            copy(
+                out=w_grp[i][:].rearrange("p (t m j) -> p t m j", t=4, j=PACK)[:, t0:t1],
+                in_=w_raw[i][:].rearrange("p (j m t) -> p t m j", j=PACK, t=4)[:, t0:t1],
+            )
+
+        def quantise_w_half(i, h):
+            nc.vector.quantize_mx(
+                out=w_code[i][:, h * 2 * P : (h + 1) * 2 * P].bitcast(FP8X4),
+                scales=w_scale[i][:, h * 2 * P : (h + 1) * 2 * P],
+                in_=w_grp[i][:, h * 2 * CD : (h + 1) * 2 * CD],
+            )
 
         def quantise_w(i):
             nc.vector.quantize_mx(out=w_code[i][:].bitcast(FP8X4), scales=w_scale[i][:], in_=w_grp[i][:])
@@ -180,8 +201,8 @@ def tile_spectralchannelmixing_kernel(tc, x, wc, out):
         nc.scalar.activation(out=warm[:], in_=warm[:], func=GELU)
 
         load_x_one(0)
-        load_x_one(1)
         load_w(0)
+        load_x_one(1)
         load_x_pair(2)
         for i in range(1, CB):
             load_w(i)
@@ -190,17 +211,18 @@ def tile_spectralchannelmixing_kernel(tc, x, wc, out):
 
         regroup_x_scalar(0)
         regroup_x_vector(0)
+        quantise_x(0)
+        regroup_w_tiles(nc.vector.tensor_copy, 0, 0, 2)
+        regroup_w_tiles(nc.scalar.copy, 0, 2, 4)
         regroup_x_scalar(1)
         regroup_x_vector(1)
-        quantise_x(0)
+        quantise_w_half(0, 0)
+        quantise_w_half(0, 1)
         quantise_x(1)
-        regroup_w(nc.vector.tensor_copy, 0, 0, W0_VECTOR_M)
-        regroup_w(nc.scalar.copy, 0, W0_VECTOR_M, P)
-        regroup_x_scalar(2)
-        regroup_x_vector(2)
-        quantise_w(0)
         multiply(0)
         multiply(1)
+        regroup_x_scalar(2)
+        regroup_x_vector(2)
         regroup_x_scalar(3)
         regroup_x_vector(3)
         for n in range(4, W_LEAD):
@@ -223,5 +245,6 @@ def tile_spectralchannelmixing_kernel(tc, x, wc, out):
                 multiply(a + 2)
                 multiply(b + 2)
             regroup_x_pool(b + 4)
+            regroup_x_pool(a + 6)
             finish(a)
             finish(b)

@@ -1,6 +1,7 @@
 from contextlib import ExitStack
 
 import concourse.mybir as mybir
+from concourse.masks import make_identity
 
 BF16 = mybir.dt.bfloat16
 F32 = mybir.dt.float32
@@ -27,6 +28,7 @@ W_LEAD = 6
 FINE_GELU = 4
 FIRST_POOL_SLAB = 5
 FIRST_SHARED_SLAB = 6
+FIRST_TURNED_BLOCK = 2
 LAST_CUTS = (0, 512, 768, 1024)
 
 
@@ -53,7 +55,8 @@ def tile_spectralchannelmixing_kernel(tc, x, wc, out):
     with ExitStack() as ctx:
         keep = ctx.enter_context(tc.tile_pool(name="keep", bufs=1))
         stage = ctx.enter_context(tc.tile_pool(name="stage", bufs=1))
-        banks = ctx.enter_context(tc.psum_pool(name="banks", bufs=8))
+        banks = ctx.enter_context(tc.psum_pool(name="banks", bufs=6))
+        turns = ctx.enter_context(tc.psum_pool(name="turns", bufs=2))
         ctx.enter_context(tc.manual_schedule())
 
         w_raw = [keep.tile([P, PACK * CD], BF16, name="w_raw%d" % i) for i in range(CB)]
@@ -66,6 +69,7 @@ def tile_spectralchannelmixing_kernel(tc, x, wc, out):
         x_raw = []
         x_grp = {}
         acc = {}
+        turned = {}
 
         def channels(i):
             return slice(i * CD, (i + 1) * CD)
@@ -133,8 +137,27 @@ def tile_spectralchannelmixing_kernel(tc, x, wc, out):
             )
 
         def regroup_w_quarter(n):
-            if n < 4 * CB:
+            if n < 4 * FIRST_TURNED_BLOCK:
                 regroup_w(nc.scalar.copy, n // 4, 32 * (n % 4), 32 * (n % 4) + 32)
+
+        def turn_w_half(n):
+            if 2 * FIRST_TURNED_BLOCK <= n < 2 * CB:
+                bank = turns.tile([P, 2 * CD], BF16, name="turn", tag="turn")
+                turned[n] = bank
+                src = w_raw[n // 2][:].rearrange("p (j m t) -> p t m j", j=PACK, t=4)
+                for e in range(2):
+                    nc.tensor.matmul(
+                        out=bank[:, e * CD : (e + 1) * CD].rearrange("p (m j) -> p m j", j=PACK),
+                        lhsT=ident[:],
+                        rhs=src[:, 2 * (n % 2) + e],
+                        start=True,
+                        stop=True,
+                    )
+
+        def collect_w_half(n):
+            if 2 * FIRST_TURNED_BLOCK <= n < 2 * CB:
+                cols = slice((n % 2) * 2 * CD, (n % 2 + 1) * 2 * CD)
+                nc.scalar.copy(out=w_grp[n // 2][:, cols], in_=turned[n][:])
 
         def regroup_w_tiles(copy, i, t0, t1):
             copy(
@@ -196,6 +219,8 @@ def tile_spectralchannelmixing_kernel(tc, x, wc, out):
             if v < NV - 1:
                 nc.sync.dma_start(out=dst, in_=res[v][:])
 
+        ident = keep.tile([P, P], BF16, name="ident")
+        make_identity(nc, ident[:])
         warm = keep.tile([P, 1], F32, name="warm")
         nc.vector.memset(warm[:], 0.0)
         nc.scalar.activation(out=warm[:], in_=warm[:], func=GELU)
@@ -233,6 +258,7 @@ def tile_spectralchannelmixing_kernel(tc, x, wc, out):
             regroup_x_scalar(a + 4)
             regroup_w_quarter(W_LEAD + a)
             regroup_w_quarter(W_LEAD + a + 1)
+            collect_w_half(3 + a // 2)
             if a == 2:
                 regroup_x_vector(4)
             if a >= 2:
@@ -243,8 +269,10 @@ def tile_spectralchannelmixing_kernel(tc, x, wc, out):
                 quantise_x(a + 2)
                 quantise_x(b + 2)
                 multiply(a + 2)
-                multiply(b + 2)
             regroup_x_pool(b + 4)
             regroup_x_pool(a + 6)
             finish(a)
+            if a + 2 < NV:
+                multiply(b + 2)
+            turn_w_half(4 + a // 2)
             finish(b)

@@ -29,7 +29,17 @@ FINE_GELU = 4
 FIRST_POOL_SLAB = 5
 FIRST_SHARED_SLAB = 6
 FIRST_TURNED_BLOCK = 2
+TURNED_SLABS = (6, 8, 10)
+TURN_ORDER = ("x6", "w4", "x8", "w5", "x10", "w6", "w7")
 LAST_CUTS = (0, 512, 768, 1024)
+TURNS_A = {}
+TURNS_B = {0: (0, 1), 2: (2, 3), 4: (4, 5), 6: (6,)}
+COLLECTS = {2: (0, 1), 4: (2, 3), 6: (4, 5), 8: (6,)}
+COLLECTS_LATE = {}
+COLLECTS_MID = {}
+
+
+SG = {0: 20, 1: 20, 2: 24, 3: 24, 4: 24, 12: 24, 14: 24}
 
 
 def on_pool(v):
@@ -43,11 +53,9 @@ def pool_groups(v):
 
 
 def scalar_groups(v):
-    if v < 2:
-        return 20
-    if pool_groups(v) > 0:
-        return 16
-    return 24
+    if v in TURNED_SLABS:
+        return 0
+    return SG[v]
 
 
 def tile_spectralchannelmixing_kernel(tc, x, wc, out):
@@ -114,7 +122,7 @@ def tile_spectralchannelmixing_kernel(tc, x, wc, out):
                 regroup_x(nc.scalar.copy, v, GROUPS - scalar_groups(v), GROUPS)
 
         def regroup_x_vector(v):
-            if v < NV and not on_pool(v):
+            if v < NV and not on_pool(v) and v not in TURNED_SLABS and GROUPS > scalar_groups(v) + pool_groups(v):
                 regroup_x(nc.vector.tensor_copy, v, 0, GROUPS - scalar_groups(v) - pool_groups(v))
 
         def regroup_x_pool(v):
@@ -140,24 +148,38 @@ def tile_spectralchannelmixing_kernel(tc, x, wc, out):
             if n < 4 * FIRST_TURNED_BLOCK:
                 regroup_w(nc.scalar.copy, n // 4, 32 * (n % 4), 32 * (n % 4) + 32)
 
-        def turn_w_half(n):
-            if 2 * FIRST_TURNED_BLOCK <= n < 2 * CB:
-                bank = turns.tile([P, 2 * CD], BF16, name="turn", tag="turn")
-                turned[n] = bank
-                src = w_raw[n // 2][:].rearrange("p (j m t) -> p t m j", j=PACK, t=4)
-                for e in range(2):
-                    nc.tensor.matmul(
-                        out=bank[:, e * CD : (e + 1) * CD].rearrange("p (m j) -> p m j", j=PACK),
-                        lhsT=ident[:],
-                        rhs=src[:, 2 * (n % 2) + e],
-                        start=True,
-                        stop=True,
-                    )
+        def turn(k):
+            if k >= len(TURN_ORDER):
+                return
+            unit = TURN_ORDER[k]
+            n = int(unit[1:])
+            bank = turns.tile([P, 2 * CD], BF16, name="turn", tag="turn")
+            turned[k] = bank
+            for e in range(2):
+                if unit[0] == "w":
+                    width = CD
+                    src = w_raw[n // 2][:].rearrange("p (j m t) -> p t m j", j=PACK, t=4)[:, 2 * (n % 2) + e]
+                else:
+                    width = 2 * (HW - 4 * pool_groups(n))
+                    src = x_raw[n].rearrange("p (t q) -> p q t", t=PACK)[:, e * width // PACK : (e + 1) * width // PACK]
+                nc.tensor.matmul(
+                    out=bank[:, e * width : (e + 1) * width].rearrange("p (m j) -> p m j", j=PACK),
+                    lhsT=ident[:],
+                    rhs=src,
+                    start=True,
+                    stop=True,
+                )
 
-        def collect_w_half(n):
-            if 2 * FIRST_TURNED_BLOCK <= n < 2 * CB:
-                cols = slice((n % 2) * 2 * CD, (n % 2 + 1) * 2 * CD)
-                nc.scalar.copy(out=w_grp[n // 2][:, cols], in_=turned[n][:])
+        def collect(k):
+            if k >= len(TURN_ORDER):
+                return
+            unit = TURN_ORDER[k]
+            n = int(unit[1:])
+            if unit[0] == "w":
+                nc.scalar.copy(out=w_grp[n // 2][:, (n % 2) * 2 * CD : (n % 2 + 1) * 2 * CD], in_=turned[k][:])
+            else:
+                width = PACK * (HW - 4 * pool_groups(n))
+                nc.scalar.copy(out=grouped(n)[:, 0:width], in_=turned[k][:, 0:width])
 
         def regroup_w_tiles(copy, i, t0, t1):
             copy(
@@ -258,7 +280,8 @@ def tile_spectralchannelmixing_kernel(tc, x, wc, out):
             regroup_x_scalar(a + 4)
             regroup_w_quarter(W_LEAD + a)
             regroup_w_quarter(W_LEAD + a + 1)
-            collect_w_half(3 + a // 2)
+            for k in COLLECTS.get(a, ()):
+                collect(k)
             if a == 2:
                 regroup_x_vector(4)
             if a >= 2:
@@ -269,10 +292,17 @@ def tile_spectralchannelmixing_kernel(tc, x, wc, out):
                 quantise_x(a + 2)
                 quantise_x(b + 2)
                 multiply(a + 2)
+            for k in TURNS_A.get(a, ()):
+                turn(k)
+            for k in COLLECTS_LATE.get(a, ()):
+                collect(k)
             regroup_x_pool(b + 4)
             regroup_x_pool(a + 6)
             finish(a)
+            for k in COLLECTS_MID.get(a, ()):
+                collect(k)
             if a + 2 < NV:
                 multiply(b + 2)
-            turn_w_half(4 + a // 2)
+            for k in TURNS_B.get(a, ()):
+                turn(k)
             finish(b)

@@ -30,13 +30,13 @@ FIRST_POOL_SLAB = 5
 FIRST_SHARED_SLAB = 6
 FIRST_TURNED_BLOCK = 2
 TURNED_SLABS = (6, 8, 10)
-TURN_ORDER = ("x6", "w4", "x8", "w5", "x10", "w6", "w7")
+TURN_ORDER = ("x6", "w4", "w5", "x8", "x10", "w6", "w7")
 LAST_CUTS = (0, 512, 768, 1024)
-TURNS_A = {}
-TURNS_B = {0: (0, 1), 2: (2, 3), 4: (4, 5), 6: (6,)}
-COLLECTS = {2: (0, 1), 4: (2, 3), 6: (4, 5), 8: (6,)}
+TURNS_A = {2: (2,)}
+TURNS_B = {0: (0, 1), 2: (3,), 4: (4, 5), 6: (6,)}
+COLLECTS = {2: (0, 1), 4: (3,), 6: (4, 5), 8: (6,)}
 COLLECTS_LATE = {}
-COLLECTS_MID = {}
+COLLECTS_MID = {2: (2,)}
 
 
 SG = {0: 20, 1: 20, 2: 24, 3: 24, 4: 24, 12: 24, 14: 24}
@@ -105,7 +105,7 @@ def tile_spectralchannelmixing_kernel(tc, x, wc, out):
 
         def grouped(v):
             if v not in x_grp:
-                if v % 2 == 1:
+                if v % 2 == 1 and v > 1:
                     x_grp[v] = stage.tile([P, SLAB], BF16, name="odd_grp", tag="odd_grp", align_bytes=64)
                 else:
                     x_grp[v] = keep.tile([P, SLAB], BF16, name="x_grp%d" % v, align_bytes=64)
@@ -265,11 +265,11 @@ def tile_spectralchannelmixing_kernel(tc, x, wc, out):
         regroup_x_vector(1)
         quantise_w_half(0, 0)
         quantise_w_half(0, 1)
-        quantise_x(1)
         multiply(0)
-        multiply(1)
         regroup_x_scalar(2)
         regroup_x_vector(2)
+        quantise_x(1)
+        multiply(1)
         regroup_x_scalar(3)
         regroup_x_vector(3)
         for n in range(4, W_LEAD):
@@ -277,9 +277,9 @@ def tile_spectralchannelmixing_kernel(tc, x, wc, out):
 
         for a in range(0, NV, 2):
             b = a + 1
-            regroup_x_scalar(a + 4)
             regroup_w_quarter(W_LEAD + a)
             regroup_w_quarter(W_LEAD + a + 1)
+            regroup_x_scalar(a + 4)
             for k in COLLECTS.get(a, ()):
                 collect(k)
             if a == 2:

from contextlib import ExitStack

import concourse.mybir as mybir
from concourse.masks import make_identity

BF16 = mybir.dt.bfloat16
F32 = mybir.dt.float32
U32 = mybir.dt.uint32
U8 = mybir.dt.uint8
FP8X4 = mybir.dt.float8_e4m3fn_x4
GELU = mybir.ActivationFunctionType.Gelu
ADD = mybir.AluOpType.add
MULT = mybir.AluOpType.mult

P = 128
B = 4
CB = 4
CD = 512
HW = 256
PACK = 4
NV = B * CB
SLAB = PACK * HW
GROUPS = HW // 4

FLOPS = 2 * CB * B * HW * CD * CD

W_LEAD = 6
FINE_GELU = 4
FIRST_POOL_SLAB = 5
FIRST_SHARED_SLAB = 6
FIRST_TURNED_BLOCK = 2
TURNED_SLABS = (6, 8, 10)
TURN_ORDER = ("x6", "w4", "w5", "x8", "x10", "w6", "w7")
LAST_CUTS = (0, 512, 768, 1024)
TURNS_A = {2: (2,)}
TURNS_B = {0: (0, 1), 2: (3,), 4: (4, 5), 6: (6,)}
COLLECTS = {2: (0, 1), 4: (3,), 6: (4, 5), 8: (6,)}
COLLECTS_LATE = {}
COLLECTS_MID = {2: (2,)}


SG = {0: 20, 1: 20, 2: 24, 3: 24, 4: 24, 12: 24, 14: 24}


def on_pool(v):
    return v % 2 == 1 and v >= FIRST_POOL_SLAB


def pool_groups(v):
    if v % 2 == 0 and v >= FIRST_SHARED_SLAB:
        return 24
    return 0


def scalar_groups(v):
    if v in TURNED_SLABS:
        return 0
    return SG[v]


def tile_spectralchannelmixing_kernel(tc, x, wc, out):
    nc = tc.nc
    with ExitStack() as ctx:
        keep = ctx.enter_context(tc.tile_pool(name="keep", bufs=1))
        stage = ctx.enter_context(tc.tile_pool(name="stage", bufs=1))
        banks = ctx.enter_context(tc.psum_pool(name="banks", bufs=6))
        turns = ctx.enter_context(tc.psum_pool(name="turns", bufs=2))
        ctx.enter_context(tc.manual_schedule())

        w_raw = [keep.tile([P, PACK * CD], BF16, name="w_raw%d" % i) for i in range(CB)]
        w_grp = [keep.tile([P, PACK * CD], BF16, name="w_grp%d" % i, align_bytes=64) for i in range(CB)]
        w_code = [keep.tile([P, CD], U32, name="w_code%d" % i, align_bytes=64) for i in range(CB)]
        w_scale = [keep.tile([P, CD], U8, name="w_scale%d" % i, align_bytes=64) for i in range(CB)]
        x_code = [keep.tile([P, HW], U32, name="x_code%d" % v, align_bytes=64) for v in range(NV)]
        x_scale = [keep.tile([P, HW], U8, name="x_scale%d" % v, align_bytes=64) for v in range(NV)]
        res = [keep.tile([P, SLAB], F32, name="res%d" % v) for v in range(NV)]
        x_raw = []
        x_grp = {}
        acc = {}
        turned = {}

        def channels(i):
            return slice(i * CD, (i + 1) * CD)

        def load_w(i):
            nc.sync.dma_start(out=w_raw[i][:], in_=wc[i].rearrange("(p j) o -> p (j o)", j=PACK))

        def load_x_one(v):
            one = keep.tile([P, SLAB], BF16, name="x_raw%d" % v)
            nc.sync.dma_start(
                out=one[:],
                in_=x[v % B, channels(v // B)].rearrange("(p j) h w -> p (j h w)", j=PACK),
            )
            x_raw.append(one[:])

        def load_x_pair(v):
            pair = keep.tile([P, 2, SLAB], BF16, name="x_raw%d" % v)
            b = v % B
            nc.sync.dma_start(
                out=pair[:],
                in_=x[b : b + 2, channels(v // B)].rearrange("b (p j) h w -> p b (j h w)", j=PACK),
            )
            x_raw.append(pair[:, 0, :])
            x_raw.append(pair[:, 1, :])

        def grouped(v):
            if v not in x_grp:
                if v % 2 == 1 and v > 1:
                    x_grp[v] = stage.tile([P, SLAB], BF16, name="odd_grp", tag="odd_grp", align_bytes=64)
                else:
                    x_grp[v] = keep.tile([P, SLAB], BF16, name="x_grp%d" % v, align_bytes=64)
            return x_grp[v]

        def regroup_x(copy, v, c0, c1):
            copy(
                out=grouped(v)[:].rearrange("p (c i t) -> p c t i", i=4, t=PACK)[:, c0:c1],
                in_=x_raw[v].rearrange("p (t c i) -> p c t i", t=PACK, i=4)[:, c0:c1],
            )

        def regroup_x_scalar(v):
            if v < NV and not on_pool(v) and scalar_groups(v) > 0:
                regroup_x(nc.scalar.copy, v, GROUPS - scalar_groups(v), GROUPS)

        def regroup_x_vector(v):
            if v < NV and not on_pool(v) and v not in TURNED_SLABS and GROUPS > scalar_groups(v) + pool_groups(v):
                regroup_x(nc.vector.tensor_copy, v, 0, GROUPS - scalar_groups(v) - pool_groups(v))

        def regroup_x_pool(v):
            if v < NV and (on_pool(v) or pool_groups(v) > 0):
                q1 = HW if on_pool(v) else 4 * (GROUPS - scalar_groups(v))
                q0 = 0 if on_pool(v) else q1 - 4 * pool_groups(v)
                nc.gpsimd.tensor_scalar(
                    out=grouped(v)[:].rearrange("p (q t) -> p q t", t=PACK)[:, q0:q1],
                    in0=x_raw[v].rearrange("p (t q) -> p q t", t=PACK)[:, q0:q1],
                    scalar1=1.0,
                    scalar2=0.0,
                    op0=MULT,
                    op1=ADD,
                )

        def regroup_w(copy, i, m0, m1):
            copy(
                out=w_grp[i][:].rearrange("p (t m j) -> p m j t", t=4, j=PACK)[:, m0:m1],
                in_=w_raw[i][:].rearrange("p (j m t) -> p m j t", j=PACK, t=4)[:, m0:m1],
            )

        def regroup_w_quarter(n):
            if n < 4 * FIRST_TURNED_BLOCK:
                regroup_w(nc.scalar.copy, n // 4, 32 * (n % 4), 32 * (n % 4) + 32)

        def turn(k):
            if k >= len(TURN_ORDER):
                return
            unit = TURN_ORDER[k]
            n = int(unit[1:])
            bank = turns.tile([P, 2 * CD], BF16, name="turn", tag="turn")
            turned[k] = bank
            for e in range(2):
                if unit[0] == "w":
                    width = CD
                    src = w_raw[n // 2][:].rearrange("p (j m t) -> p t m j", j=PACK, t=4)[:, 2 * (n % 2) + e]
                else:
                    width = 2 * (HW - 4 * pool_groups(n))
                    src = x_raw[n].rearrange("p (t q) -> p q t", t=PACK)[:, e * width // PACK : (e + 1) * width // PACK]
                nc.tensor.matmul(
                    out=bank[:, e * width : (e + 1) * width].rearrange("p (m j) -> p m j", j=PACK),
                    lhsT=ident[:],
                    rhs=src,
                    start=True,
                    stop=True,
                )

        def collect(k):
            if k >= len(TURN_ORDER):
                return
            unit = TURN_ORDER[k]
            n = int(unit[1:])
            if unit[0] == "w":
                nc.scalar.copy(out=w_grp[n // 2][:, (n % 2) * 2 * CD : (n % 2 + 1) * 2 * CD], in_=turned[k][:])
            else:
                width = PACK * (HW - 4 * pool_groups(n))
                nc.scalar.copy(out=grouped(n)[:, 0:width], in_=turned[k][:, 0:width])

        def regroup_w_tiles(copy, i, t0, t1):
            copy(
                out=w_grp[i][:].rearrange("p (t m j) -> p t m j", t=4, j=PACK)[:, t0:t1],
                in_=w_raw[i][:].rearrange("p (j m t) -> p t m j", j=PACK, t=4)[:, t0:t1],
            )

        def quantise_w_half(i, h):
            nc.vector.quantize_mx(
                out=w_code[i][:, h * 2 * P : (h + 1) * 2 * P].bitcast(FP8X4),
                scales=w_scale[i][:, h * 2 * P : (h + 1) * 2 * P],
                in_=w_grp[i][:, h * 2 * CD : (h + 1) * 2 * CD],
            )

        def quantise_w(i):
            nc.vector.quantize_mx(out=w_code[i][:].bitcast(FP8X4), scales=w_scale[i][:], in_=w_grp[i][:])

        def quantise_x(v):
            nc.vector.quantize_mx(out=x_code[v][:].bitcast(FP8X4), scales=x_scale[v][:], in_=grouped(v)[:])

        def multiply(v):
            i = v // B
            for h in range(2):
                bank = banks.tile([P, 2 * HW], F32, name="acc", tag="acc")
                acc[(v, h)] = bank
                for e in range(2):
                    cols = slice((2 * h + e) * P, (2 * h + e + 1) * P)
                    nc.tensor.matmul_mx(
                        out=bank[:, e * HW : (e + 1) * HW],
                        lhsT=w_code[i][:, cols].bitcast(FP8X4),
                        lhsT_scale=w_scale[i][:, cols],
                        rhs=x_code[v][:].bitcast(FP8X4),
                        rhs_scale=x_scale[v][:],
                        start=True,
                        stop=True,
                    )

        def finish(v):
            dst = out[v % B, channels(v // B)].rearrange("(p t) h w -> p (t h w)", t=4)
            half = SLAB // 2
            if v == NV - 1:
                cuts = LAST_CUTS
            elif v >= NV - FINE_GELU:
                cuts = (0, half, SLAB)
            else:
                cuts = (0, SLAB)
            add_cuts = sorted(set(cuts + (half,)))
            for lo, hi in zip(add_cuts[:-1], add_cuts[1:]):
                nc.vector.tensor_tensor(
                    out=res[v][:, lo:hi],
                    in0=acc[(v, lo // half)][:, lo % half : lo % half + hi - lo],
                    in1=x_raw[v][:, lo:hi],
                    op=ADD,
                )
            for lo, hi in zip(cuts[:-1], cuts[1:]):
                nc.scalar.activation(out=res[v][:, lo:hi], in_=res[v][:, lo:hi], func=GELU)
                if v == NV - 1:
                    nc.sync.dma_start(out=dst[:, lo:hi], in_=res[v][:, lo:hi])
            if v < NV - 1:
                nc.sync.dma_start(out=dst, in_=res[v][:])

        ident = keep.tile([P, P], BF16, name="ident")
        make_identity(nc, ident[:])
        warm = keep.tile([P, 1], F32, name="warm")
        nc.vector.memset(warm[:], 0.0)
        nc.scalar.activation(out=warm[:], in_=warm[:], func=GELU)

        load_x_one(0)
        load_w(0)
        load_x_one(1)
        load_x_pair(2)
        for i in range(1, CB):
            load_w(i)
            load_x_pair(B * i)
            load_x_pair(B * i + 2)

        regroup_x_scalar(0)
        regroup_x_vector(0)
        quantise_x(0)
        regroup_w_tiles(nc.vector.tensor_copy, 0, 0, 2)
        regroup_w_tiles(nc.scalar.copy, 0, 2, 4)
        regroup_x_scalar(1)
        regroup_x_vector(1)
        quantise_w_half(0, 0)
        quantise_w_half(0, 1)
        multiply(0)
        regroup_x_scalar(2)
        regroup_x_vector(2)
        quantise_x(1)
        multiply(1)
        regroup_x_scalar(3)
        regroup_x_vector(3)
        for n in range(4, W_LEAD):
            regroup_w_quarter(n)

        for a in range(0, NV, 2):
            b = a + 1
            regroup_w_quarter(W_LEAD + a)
            regroup_w_quarter(W_LEAD + a + 1)
            regroup_x_scalar(a + 4)
            for k in COLLECTS.get(a, ()):
                collect(k)
            if a == 2:
                regroup_x_vector(4)
            if a >= 2:
                regroup_x_vector(a + 4)
            if a + 2 < NV:
                if (a + 2) % B == 0:
                    quantise_w((a + 2) // B)
                quantise_x(a + 2)
                quantise_x(b + 2)
                multiply(a + 2)
            for k in TURNS_A.get(a, ()):
                turn(k)
            for k in COLLECTS_LATE.get(a, ()):
                collect(k)
            regroup_x_pool(b + 4)
            regroup_x_pool(a + 6)
            finish(a)
            for k in COLLECTS_MID.get(a, ()):
                collect(k)
            if a + 2 < NV:
                multiply(b + 2)
            for k in TURNS_B.get(a, ()):
                turn(k)
            finish(b)
